import numpy as np
import ml_dtypes


def mxq(x, axis, fmt="e4m3"):
    dtype, down = {"e4m3": (ml_dtypes.float8_e4m3fn, 7), "e5m2": (ml_dtypes.float8_e5m2, 14)}[fmt]
    v = np.moveaxis(np.asarray(x, np.float32).astype(ml_dtypes.bfloat16).astype(np.float64), axis, -1)
    blocks = v.reshape(v.shape[:-1] + (-1, 32))
    amax = np.abs(blocks).max(-1, keepdims=True)
    byte = np.maximum(np.where(amax > 0, np.frexp(amax)[1] - 1 + 127, 0) - down, 1)
    scale = np.exp2(byte - 127.0)
    codes = (blocks / scale).astype(np.float32).astype(dtype).astype(np.float64)
    return np.moveaxis((codes * scale).reshape(v.shape), -1, axis)


WIDE = False


def mx_kscale(k):
    if not WIDE:
        return np.ones(k)
    levels = np.array([10, -10, 5, -5, 0])
    a = np.random.permutation(np.resize(levels, k // 512 * 4)).reshape(k // 512, 4)
    idx = np.arange(k)
    return np.exp2(a[idx // 512, idx % 128 // 32])


BF16 = ml_dtypes.bfloat16


def bf(x):
    return np.asarray(x, np.float32).astype(BF16)


def f64(x):
    return np.asarray(x).astype(np.float64)


E2M1 = np.array([0.0, 0.5, 1.0, 1.5, 2.0, 3.0, 4.0, 6.0, -0.0, -0.5, -1.0, -1.5, -2.0, -3.0, -4.0, -6.0])


def pack_weight(w, fmt):
    k, n = w.shape
    w = f64(bf(w)).reshape(k // 32, 32, n)
    amax = np.abs(w).max(1)
    if fmt == "e4m3":
        byte = np.frexp(amax)[1] - 1 + 127 - 7
    else:
        mant, ex = np.frexp(amax / 6.0)
        byte = np.where(mant > 0.5, ex, ex - 1) + 127
    byte = np.clip(np.where(amax > 0, byte, 1), 1, 254)
    scaled = (w * np.exp2(127.0 - byte)[:, None, :]).reshape(k, n).astype(np.float32)
    by_word = np.ascontiguousarray(scaled.reshape(k // 512, 128, 4, n).transpose(0, 1, 3, 2))
    if fmt == "e4m3":
        words = by_word.astype(ml_dtypes.float8_e4m3fn).view(np.uint8)
    else:
        c = by_word.astype(ml_dtypes.float4_e2m1fn).view(np.uint8) & 0xF
        words = c[..., 0::2] | (c[..., 1::2] << 4)
    return np.ascontiguousarray(words), np.ascontiguousarray(byte.astype(np.uint8).reshape(k // 512, 16, n))


def unpack_weight(words, scales, fmt):
    g, p, n, _ = words.shape
    if fmt == "e4m3":
        vals = np.ascontiguousarray(words).view(ml_dtypes.float8_e4m3fn).astype(np.float64)
    else:
        nib = np.empty((g, p, n, 4), np.uint8)
        nib[..., 0::2] = words & 0xF
        nib[..., 1::2] = words >> 4
        vals = E2M1[nib]
    vals = vals * np.repeat(np.exp2(scales.astype(np.float64) - 127.0), 8, axis=1)[..., None]
    return vals.transpose(0, 1, 3, 2).reshape(g * 512, n)


B, T, D, E, F, H = 2, 128, 1024, 8, 512, 256
N = B * T
EF = E * F


def silu(v):
    return v / (1.0 + np.exp(-v))


def setup_inputs():
    s = mx_kscale(D)
    t = mx_kscale(EF).reshape(E, F)
    er = np.exp(np.random.standard_normal((N, E)))
    x = bf(np.random.standard_normal((B, T, D)) * s)
    r = bf(er / er.sum(-1, keepdims=True))
    Wg = np.random.standard_normal((E, D, F)) / np.sqrt(D) / s[None, :, None]
    Wu = np.random.standard_normal((E, D, F)) / np.sqrt(D) / s[None, :, None] * t[:, None, :]
    Wd = np.random.standard_normal((E, F, D)) * 1.5 / np.sqrt(F) / t[:, :, None]
    Wg_words, Wg_scales = pack_weight(Wg.reshape(-1, F), "e4m3")
    Wu_words, Wu_scales = pack_weight(Wu.reshape(-1, F), "e4m3")
    Wd_words, Wd_scales = pack_weight(Wd.reshape(-1, D), "e4m3")
    return {"x": x,
            "r": r,
            "Wg_words": Wg_words, "Wg_scales": Wg_scales,
            "Wu_words": Wu_words, "Wu_scales": Wu_scales,
            "Wd_words": Wd_words, "Wd_scales": Wd_scales}


def reference(x, r, Wg_words, Wg_scales, Wu_words, Wu_scales, Wd_words, Wd_scales):
    xq = mxq(f64(x).reshape(N, D), 1, "e4m3")
    g = silu(xq @ unpack_weight(Wg_words, Wg_scales, "e4m3").reshape(E, D, F))
    u = xq @ unpack_weight(Wu_words, Wu_scales, "e4m3").reshape(E, D, F)
    w = f64(r).T[:, :, None] * (g * u)
    w = np.swapaxes(w, 0, 1).reshape(N, EF)
    y = mxq(w, 1, "e4m3") @ unpack_weight(Wd_words, Wd_scales, "e4m3").reshape(E, F, D).reshape(EF, D)
    return y.reshape(B, T, D)

@@ -1,0 +1,228 @@
+from contextlib import ExitStack
+
+import concourse.mybir as mybir
+from concourse.masks import make_identity
+
+F32 = mybir.dt.float32
+BF16 = mybir.dt.bfloat16
+I32 = mybir.dt.int32
+U32 = mybir.dt.uint32
+U8 = mybir.dt.uint8
+FP8X4 = mybir.dt.float8_e4m3fn_x4
+SILU = mybir.ActivationFunctionType.Silu
+MULT = mybir.AluOpType.mult
+
+P = 128
+PACK = 4
+K_PASS = P * PACK
+TOKEN_TILES = 2
+D = 1024
+E = 8
+F = 512
+X_PASSES = D // K_PASS
+BANK = 512
+D_HALVES = D // BANK
+QUADRANTS = 4
+PLANES = 4
+
+FLOPS = 2 * TOKEN_TILES * P * E * (2 * D * F + F * D)
+
+
+def tile_moelayer_pa_e_kernel(
+    tc, x, r, Wg_words, Wg_scales, Wu_words, Wu_scales, Wd_words, Wd_scales, out
+):
+    nc = tc.nc
+    with ExitStack() as ctx:
+        keep = ctx.enter_context(tc.tile_pool(name="keep", bufs=1))
+        work = ctx.enter_context(tc.tile_pool(name="work", bufs=3))
+        mixed_pool = ctx.enter_context(tc.tile_pool(name="mixed", bufs=6))
+        sums = ctx.enter_context(tc.psum_pool(name="sums", bufs=6))
+        flips = ctx.enter_context(tc.psum_pool(name="flips", bufs=2))
+        ctx.enter_context(tc.manual_schedule())
+
+        wg_words = keep.tile([P, E * X_PASSES, F], U32, align_bytes=64)
+        wu_words = keep.tile([P, E * X_PASSES, F], U32, align_bytes=64)
+        wd_words = keep.tile([P, E, D], U32, align_bytes=64)
+        wg_planes = keep.tile([P, E * X_PASSES // PLANES, F], U8, align_bytes=64)
+        wu_planes = keep.tile([P, E * X_PASSES // PLANES, F], U8, align_bytes=64)
+        wd_planes = keep.tile([P, E // PLANES, D], U8, align_bytes=64)
+        x_rows = keep.tile([P, TOKEN_TILES, D], BF16)
+        x_grouped = keep.tile([P, TOKEN_TILES, X_PASSES, P, PACK], BF16, align_bytes=64)
+        x_codes = keep.tile([P, TOKEN_TILES, X_PASSES, P], U32, align_bytes=64)
+        x_scales = keep.tile([P, TOKEN_TILES, X_PASSES, P], U8, align_bytes=64)
+        w_codes = keep.tile([P, E, TOKEN_TILES, P], U32, align_bytes=64)
+        w_scales = keep.tile([P, E, TOKEN_TILES, P], U8, align_bytes=64)
+        r_rows = keep.tile([P, TOKEN_TILES, E], BF16)
+        r_f32 = keep.tile([P, TOKEN_TILES, E], F32)
+        ident_f32 = keep.tile([P, P], F32)
+        ident_bf16 = keep.tile([P, P], BF16)
+        table_in = keep.tile([P, 1], F32)
+        table_out = keep.tile([P, 1], F32)
+
+        nc.vector.memset(table_in[:], 0.0)
+        for planes in (wg_planes, wu_planes, wd_planes):
+            nc.vector.memset(planes[:].rearrange("p b n -> p (b n)").bitcast(I32), 0)
+        make_identity(nc, ident_f32[:])
+        make_identity(nc, ident_bf16[:])
+
+        for i in range(TOKEN_TILES):
+            nc.scalar.dma_start(out=x_rows[:, i, :], in_=x[i])
+        nc.scalar.dma_start(out=r_rows[:], in_=r.rearrange("(i p) e -> p i e", p=P))
+        nc.scalar.activation(out=table_out[:], in_=table_in[:], func=SILU)
+
+        def load_scale_rows(planes, scales, block, quadrant):
+            nc.sync.dma_start(
+                out=planes[32 * quadrant : 32 * quadrant + PLANES * 4, block, :].bitcast(I32),
+                in_=scales[
+                    PLANES * block : PLANES * (block + 1), 4 * quadrant : 4 * (quadrant + 1), :
+                ].bitcast(I32),
+            )
+
+        def load_words(words, dram_words, first, count, columns):
+            nc.sync.dma_start(
+                out=words[:, first : first + count, columns].bitcast(I32),
+                in_=dram_words[first : first + count, :, columns, :]
+                .rearrange("g p n t -> p g (n t)")
+                .bitcast(I32),
+            )
+
+        gate_up_weights = (
+            (wg_words, Wg_words, wg_planes, Wg_scales),
+            (wu_words, Wu_words, wu_planes, Wu_scales),
+        )
+        experts_per_block = PLANES // X_PASSES
+        for e in range(E):
+            for m, (words, dram_words, planes, scales) in enumerate(gate_up_weights):
+                if e == 0:
+                    for quadrant in range(QUADRANTS):
+                        load_scale_rows(planes, scales, 0, quadrant)
+                load_words(words, dram_words, X_PASSES * e, X_PASSES, slice(0, F))
+                next_block = e // experts_per_block + 1
+                for quadrant in range(2 * (e % 2), 2 * (e % 2) + 2):
+                    if next_block < E // experts_per_block:
+                        load_scale_rows(planes, scales, next_block, quadrant)
+                    else:
+                        load_scale_rows(wd_planes, Wd_scales, m, quadrant)
+        for half in range(D_HALVES):
+            for e in range(0, E, 2):
+                load_words(wd_words, Wd_words, e, 2, slice(BANK * half, BANK * (half + 1)))
+
+        for i in range(TOKEN_TILES):
+            x_pairs = x_rows[:, i, :].bitcast(F32)
+            x_flipped = flips.tile([P, X_PASSES, 2, P], F32, tag="flip")
+            for g in range(X_PASSES):
+                for u in range(2):
+                    nc.tensor.transpose(
+                        x_flipped[:, g, u, :],
+                        x_pairs[:, 256 * g + u : 256 * (g + 1) : 2],
+                        ident_f32[:],
+                    )
+            grouped_pairs = (
+                x_grouped[:, i]
+                .rearrange("p g n t -> p (g n t)")
+                .bitcast(F32)
+                .rearrange("p (g n u) -> p g n u", g=X_PASSES, u=2)
+            )
+            if i == 0:
+                nc.vector.tensor_copy(
+                    out=grouped_pairs, in_=x_flipped[:].rearrange("p g u n -> p g n u")
+                )
+            else:
+                nc.scalar.copy(out=grouped_pairs, in_=x_flipped[:].rearrange("p g u n -> p g n u"))
+        for i in range(TOKEN_TILES):
+            nc.vector.quantize_mx(
+                out=x_codes[:, i].rearrange("p g n -> p (g n)").bitcast(FP8X4),
+                scales=x_scales[:, i].rearrange("p g n -> p (g n)"),
+                in_=x_grouped[:, i].rearrange("p g n t -> p (g n t)"),
+            )
+        nc.vector.tensor_copy(out=r_f32[:], in_=r_rows[:])
+
+        def gate_and_up(e, i):
+            banks = []
+            for words, planes in ((wg_words, wg_planes), (wu_words, wu_planes)):
+                bank = sums.tile([P, F], F32, tag="sum")
+                for h in range(X_PASSES):
+                    g = X_PASSES * e + h
+                    nc.tensor.matmul_mx(
+                        out=bank[:],
+                        lhsT=x_codes[:, i, h, :].bitcast(FP8X4),
+                        lhsT_scale=x_scales[:, i, h, :],
+                        rhs=words[:, g, :].bitcast(FP8X4),
+                        rhs_scale=planes[4 * (g % PLANES) : P, g // PLANES, :],
+                        start=(h == 0),
+                        stop=(h == X_PASSES - 1),
+                    )
+                banks.append(bank)
+            return banks
+
+        def mix(e, i, gate, up):
+            gate_silu = work.tile([P, PACK, P], F32, tag="gate_silu")
+            nc.scalar.activation(
+                out=gate_silu[:], in_=gate[:].rearrange("n (p t) -> n t p", t=PACK), func=SILU
+            )
+            mixed = mixed_pool.tile([P, PACK, P], BF16, tag="mixed")
+            nc.vector.scalar_tensor_tensor(
+                out=mixed[:],
+                in0=up[:].rearrange("n (p t) -> n t p", t=PACK),
+                scalar=r_f32[:, i, e : e + 1],
+                in1=gate_silu[:],
+                op0=MULT,
+                op1=MULT,
+            )
+            return mixed
+
+        def flip_and_quantise(e, i, mixed):
+            flipped = flips.tile([P, PACK, P], BF16, tag="flip")
+            for t in range(PACK):
+                nc.tensor.transpose(flipped[:, t, :], mixed[:, t, :], ident_bf16[:])
+            grouped = work.tile([P, P, PACK], BF16, tag="grouped", align_bytes=64)
+            nc.scalar.copy(out=grouped[:], in_=flipped[:].rearrange("p t n -> p n t"))
+            nc.vector.quantize_mx(
+                out=w_codes[:, e, i, :].bitcast(FP8X4),
+                scales=w_scales[:, e, i, :],
+                in_=grouped[:].rearrange("p n t -> p (n t)"),
+            )
+
+        def down(y, i, half, experts):
+            columns = slice(BANK * half, BANK * (half + 1))
+            for e in experts:
+                nc.tensor.matmul_mx(
+                    out=y[:],
+                    lhsT=w_codes[:, e, i, :].bitcast(FP8X4),
+                    lhsT_scale=w_scales[:, e, i, :],
+                    rhs=wd_words[:, e, columns].bitcast(FP8X4),
+                    rhs_scale=wd_planes[4 * (e % PLANES) : P, e // PLANES, columns],
+                    start=(e == 0),
+                    stop=(e == E - 1),
+                )
+
+        def store(y, i, half):
+            y_rows = work.tile([P, BANK], F32, tag="y_rows")
+            if i == 0:
+                nc.vector.tensor_copy(out=y_rows[:], in_=y[:])
+            else:
+                nc.scalar.copy(out=y_rows[:], in_=y[:])
+            nc.sync.dma_start(out=out[i, :, BANK * half : BANK * (half + 1)], in_=y_rows[:])
+
+        mixed_tiles = {}
+        for e in range(E):
+            for i in range(TOKEN_TILES):
+                gate, up = gate_and_up(e, i)
+                mixed_tiles[(e, i)] = mix(e, i, gate, up)
+            if e > 0:
+                for i in range(TOKEN_TILES):
+                    flip_and_quantise(e - 1, i, mixed_tiles[(e - 1, i)])
+
+        last = E - 1
+        y_first = [sums.tile([P, BANK], F32, tag="sum", name="y_first%d" % i) for i in range(TOKEN_TILES)]
+        down(y_first[0], 0, 0, range(last))
+        for i in range(TOKEN_TILES):
+            flip_and_quantise(last, i, mixed_tiles[(last, i)])
+        down(y_first[1], 1, 0, range(last))
+        for i in range(TOKEN_TILES):
+            down(y_first[i], i, 0, [last])
+            store(y_first[i], i, 0)
+        for i in range(TOKEN_TILES):
+            y_second = sums.tile([P, BANK], F32, tag="sum")
+            down(y_second, i, 1, range(E))
+            store(y_second, i, 1)

@@ -55,7 +55,6 @@ def tile_moelayer_pa_e_kernel(
         r_rows = keep.tile([P, TOKEN_TILES, E], BF16)
         r_f32 = keep.tile([P, TOKEN_TILES, E], F32)
         ident_f32 = keep.tile([P, P], F32)
-        ident_bf16 = keep.tile([P, P], BF16)
         table_in = keep.tile([P, 1], F32)
         table_out = keep.tile([P, 1], F32)
 
@@ -63,7 +62,6 @@ def tile_moelayer_pa_e_kernel(
         for planes in (wg_planes, wu_planes, wd_planes):
             nc.vector.memset(planes[:].rearrange("p b n -> p (b n)").bitcast(I32), 0)
         make_identity(nc, ident_f32[:])
-        make_identity(nc, ident_bf16[:])
 
         for i in range(TOKEN_TILES):
             nc.scalar.dma_start(out=x_rows[:, i, :], in_=x[i])
@@ -156,27 +154,32 @@ def tile_moelayer_pa_e_kernel(
             return banks
 
         def mix(e, i, gate, up):
-            gate_silu = work.tile([P, PACK, P], F32, tag="gate_silu")
+            gate_silu = work.tile([P, 2, P, 2], F32, tag="gate_silu")
             nc.scalar.activation(
-                out=gate_silu[:], in_=gate[:].rearrange("n (p t) -> n t p", t=PACK), func=SILU
+                out=gate_silu[:], in_=gate[:].rearrange("n (p u v) -> n u p v", u=2, v=2), func=SILU
             )
-            mixed = mixed_pool.tile([P, PACK, P], BF16, tag="mixed")
-            nc.vector.scalar_tensor_tensor(
-                out=mixed[:],
-                in0=up[:].rearrange("n (p t) -> n t p", t=PACK),
-                scalar=r_f32[:, i, e : e + 1],
-                in1=gate_silu[:],
-                op0=MULT,
-                op1=MULT,
-            )
+            mixed = mixed_pool.tile([P, 2, P, 2], BF16, tag="mixed")
+            for u in range(2):
+                nc.vector.scalar_tensor_tensor(
+                    out=mixed[:, u],
+                    in0=up[:].rearrange("n (p u v) -> n u p v", u=2, v=2)[:, u],
+                    scalar=r_f32[:, i, e : e + 1],
+                    in1=gate_silu[:, u],
+                    op0=MULT,
+                    op1=MULT,
+                )
             return mixed
 
         def flip_and_quantise(e, i, mixed):
-            flipped = flips.tile([P, PACK, P], BF16, tag="flip")
-            for t in range(PACK):
-                nc.tensor.transpose(flipped[:, t, :], mixed[:, t, :], ident_bf16[:])
+            flipped = flips.tile([P, 2, P], F32, tag="flip")
+            mixed_pairs = mixed[:].rearrange("n u p v -> n (u p v)").bitcast(F32)
+            for u in range(2):
+                nc.tensor.transpose(flipped[:, u, :], mixed_pairs[:, P * u : P * (u + 1)], ident_f32[:])
             grouped = work.tile([P, P, PACK], BF16, tag="grouped", align_bytes=64)
-            nc.scalar.copy(out=grouped[:], in_=flipped[:].rearrange("p t n -> p n t"))
+            nc.scalar.copy(
+                out=grouped[:].rearrange("p n t -> p (n t)").bitcast(F32).rearrange("p (n u) -> p n u", u=2),
+                in_=flipped[:].rearrange("p u n -> p n u"),
+            )
             nc.vector.quantize_mx(
                 out=w_codes[:, e, i, :].bitcast(FP8X4),
                 scales=w_scales[:, e, i, :],

@@ -101,9 +101,13 @@ def tile_moelayer_pa_e_kernel(
                         load_scale_rows(planes, scales, next_block, quadrant)
                     else:
                         load_scale_rows(wd_planes, Wd_scales, m, quadrant)
+        wd_chunks = {
+            0: [[0, 1], [2, 3], [4, 5], [6, 7]],
+            1: [[0, 1], [2, 3], [4, 5], [6], [7]],
+        }
         for half in range(D_HALVES):
-            for e in range(0, E, 2):
-                load_words(wd_words, Wd_words, e, 2, slice(BANK * half, BANK * (half + 1)))
+            for chunk in wd_chunks[half]:
+                load_words(wd_words, Wd_words, chunk[0], len(chunk), slice(BANK * half, BANK * (half + 1)))
 
         for i in range(TOKEN_TILES):
             x_pairs = x_rows[:, i, :].bitcast(F32)
@@ -217,15 +221,17 @@ def tile_moelayer_pa_e_kernel(
                     flip_and_quantise(e - 1, i, mixed_tiles[(e - 1, i)])
 
         last = E - 1
-        y_first = [sums.tile([P, BANK], F32, tag="sum", name="y_first%d" % i) for i in range(TOKEN_TILES)]
-        down(y_first[0], 0, 0, range(last))
-        for i in range(TOKEN_TILES):
-            flip_and_quantise(last, i, mixed_tiles[(last, i)])
-        down(y_first[1], 1, 0, range(last))
-        for i in range(TOKEN_TILES):
-            down(y_first[i], i, 0, [last])
-            store(y_first[i], i, 0)
-        for i in range(TOKEN_TILES):
-            y_second = sums.tile([P, BANK], F32, tag="sum")
-            down(y_second, i, 1, range(E))
-            store(y_second, i, 1)
+        flip_before = [4, 5]
+        for half in range(D_HALVES):
+            y_banks = [
+                sums.tile([P, BANK], F32, tag="sum", name="y%d%d" % (half, i)) for i in range(TOKEN_TILES)
+            ]
+            for chunk in wd_chunks[half]:
+                if half == 0 and chunk == flip_before:
+                    for i in range(TOKEN_TILES):
+                        flip_and_quantise(last, i, mixed_tiles[(last, i)])
+                for e in chunk:
+                    for i in range(TOKEN_TILES):
+                        down(y_banks[i], i, half, [e])
+            for i in range(TOKEN_TILES):
+                store(y_banks[i], i, half)

@@ -23,6 +23,7 @@ X_PASSES = D // K_PASS
 BANK = 512
 D_HALVES = D // BANK
 QUADRANTS = 4
+T_RUN = 2
 PLANES = 4
 
 FLOPS = 2 * TOKEN_TILES * P * E * (2 * D * F + F * D)
@@ -35,7 +36,7 @@ def tile_moelayer_pa_e_kernel(
     with ExitStack() as ctx:
         keep = ctx.enter_context(tc.tile_pool(name="keep", bufs=1))
         work = ctx.enter_context(tc.tile_pool(name="work", bufs=3))
-        mixed_pool = ctx.enter_context(tc.tile_pool(name="mixed", bufs=6))
+        mixed_pool = ctx.enter_context(tc.tile_pool(name="mixed", bufs=8))
         sums = ctx.enter_context(tc.psum_pool(name="sums", bufs=6))
         flips = ctx.enter_context(tc.psum_pool(name="flips", bufs=2))
         ctx.enter_context(tc.manual_schedule())
@@ -174,21 +175,38 @@ def tile_moelayer_pa_e_kernel(
                 )
             return mixed
 
-        def flip_and_quantise(e, i, mixed):
-            flipped = flips.tile([P, 2, P], F32, tag="flip")
-            mixed_pairs = mixed[:].rearrange("n u p v -> n (u p v)").bitcast(F32)
-            for u in range(2):
-                nc.tensor.transpose(flipped[:, u, :], mixed_pairs[:, P * u : P * (u + 1)], ident_f32[:])
-            grouped = work.tile([P, P, PACK], BF16, tag="grouped", align_bytes=64)
-            nc.scalar.copy(
-                out=grouped[:].rearrange("p n t -> p (n t)").bitcast(F32).rearrange("p (n u) -> p n u", u=2),
-                in_=flipped[:].rearrange("p u n -> p n u"),
+        def flip_and_quantise(e, copy_engine):
+            flipped = flips.tile([P, TOKEN_TILES, 2, P], F32, tag="flip")
+            for i in range(TOKEN_TILES):
+                mixed_pairs = mixed_tiles[(e, i)][:].rearrange("n u p v -> n (u p v)").bitcast(F32)
+                for u in range(2):
+                    nc.tensor.transpose(
+                        flipped[:, i, u, :], mixed_pairs[:, P * u : P * (u + 1)], ident_f32[:]
+                    )
+            grouped = work.tile([P, TOKEN_TILES, P, PACK], BF16, tag="grouped", align_bytes=64)
+            grouped_pairs = (
+                grouped[:]
+                .rearrange("p i n t -> p (i n t)")
+                .bitcast(F32)
+                .rearrange("p (i n u) -> p i n u", i=TOKEN_TILES, u=2)
             )
+            if copy_engine == "scalar":
+                nc.scalar.copy(out=grouped_pairs, in_=flipped[:].rearrange("p i u n -> p i n u"))
+            else:
+                nc.vector.tensor_copy(out=grouped_pairs, in_=flipped[:].rearrange("p i u n -> p i n u"))
+            return grouped
+
+        def quantise(e, grouped):
             nc.vector.quantize_mx(
-                out=w_codes[:, e, i, :].bitcast(FP8X4),
-                scales=w_scales[:, e, i, :],
-                in_=grouped[:].rearrange("p n t -> p (n t)"),
+                out=w_codes[:, e].rearrange("p i n -> p (i n)").bitcast(FP8X4),
+                scales=w_scales[:, e].rearrange("p i n -> p (i n)"),
+                in_=grouped[:].rearrange("p i n t -> p (i n t)"),
             )
+
+        def flip_run(experts, copy_engines):
+            grouped_tiles = [flip_and_quantise(e, engine) for e, engine in zip(experts, copy_engines)]
+            for e, grouped in zip(experts, grouped_tiles):
+                quantise(e, grouped)
 
         def down(y, i, half, experts):
             columns = slice(BANK * half, BANK * (half + 1))
@@ -216,11 +234,9 @@ def tile_moelayer_pa_e_kernel(
             for i in range(TOKEN_TILES):
                 gate, up = gate_and_up(e, i)
                 mixed_tiles[(e, i)] = mix(e, i, gate, up)
-            if e > 0:
-                for i in range(TOKEN_TILES):
-                    flip_and_quantise(e - 1, i, mixed_tiles[(e - 1, i)])
+            if e >= T_RUN and e % T_RUN == 0:
+                flip_run(list(range(e - T_RUN, e)), ["scalar"] * T_RUN)
 
-        last = E - 1
         flip_before = [4, 5]
         for half in range(D_HALVES):
             y_banks = [
@@ -228,8 +244,7 @@ def tile_moelayer_pa_e_kernel(
             ]
             for chunk in wd_chunks[half]:
                 if half == 0 and chunk == flip_before:
-                    for i in range(TOKEN_TILES):
-                        flip_and_quantise(last, i, mixed_tiles[(last, i)])
+                    flip_run(list(range(E - T_RUN, E)), ["scalar", "vector"])
                 for e in chunk:
                     for i in range(TOKEN_TILES):
                         down(y_banks[i], i, half, [e])

@@ -66,7 +66,6 @@ def tile_moelayer_pa_e_kernel(
 
         for i in range(TOKEN_TILES):
             nc.scalar.dma_start(out=x_rows[:, i, :], in_=x[i])
-        nc.scalar.dma_start(out=r_rows[:], in_=r.rearrange("(i p) e -> p i e", p=P))
         nc.scalar.activation(out=table_out[:], in_=table_in[:], func=SILU)
 
         def load_scale_rows(planes, scales, block, quadrant):
@@ -90,18 +89,30 @@ def tile_moelayer_pa_e_kernel(
             (wu_words, Wu_words, wu_planes, Wu_scales),
         )
         experts_per_block = PLANES // X_PASSES
-        for e in range(E):
-            for m, (words, dram_words, planes, scales) in enumerate(gate_up_weights):
-                if e == 0:
-                    for quadrant in range(QUADRANTS):
-                        load_scale_rows(planes, scales, 0, quadrant)
+        small_loads = []
+        for block in range(E // experts_per_block):
+            for words, dram_words, planes, scales in gate_up_weights:
+                for quadrant in range(QUADRANTS):
+                    small_loads.append((planes, scales, block, quadrant))
+        for block in range(E // PLANES):
+            for quadrant in range(QUADRANTS):
+                small_loads.append((wd_planes, Wd_scales, block, quadrant))
+        for small in small_loads[:QUADRANTS]:
+            load_scale_rows(*small)
+        for words, dram_words, planes, scales in gate_up_weights:
+            load_words(words, dram_words, 0, X_PASSES, slice(0, F))
+        for small in small_loads[QUADRANTS : 2 * QUADRANTS]:
+            load_scale_rows(*small)
+        nc.sync.dma_start(out=r_rows[:], in_=r.rearrange("(i p) e -> p i e", p=P))
+        woven = small_loads[2 * QUADRANTS :]
+        for e in range(1, E):
+            for words, dram_words, planes, scales in gate_up_weights:
                 load_words(words, dram_words, X_PASSES * e, X_PASSES, slice(0, F))
-                next_block = e // experts_per_block + 1
-                for quadrant in range(2 * (e % 2), 2 * (e % 2) + 2):
-                    if next_block < E // experts_per_block:
-                        load_scale_rows(planes, scales, next_block, quadrant)
-                    else:
-                        load_scale_rows(wd_planes, Wd_scales, m, quadrant)
+                for small in woven[:2]:
+                    load_scale_rows(*small)
+                woven = woven[2:]
+        for small in woven:
+            load_scale_rows(*small)
         wd_chunks = {
             0: [[0, 1], [2, 3], [4, 5], [6, 7]],
             1: [[0, 1], [2, 3], [4, 5], [6], [7]],
@@ -140,29 +151,29 @@ def tile_moelayer_pa_e_kernel(
             )
         nc.vector.tensor_copy(out=r_f32[:], in_=r_rows[:])
 
-        def gate_and_up(e, i):
-            banks = []
-            for words, planes in ((wg_words, wg_planes), (wu_words, wu_planes)):
-                bank = sums.tile([P, F], F32, tag="sum")
-                for h in range(X_PASSES):
-                    g = X_PASSES * e + h
-                    nc.tensor.matmul_mx(
-                        out=bank[:],
-                        lhsT=x_codes[:, i, h, :].bitcast(FP8X4),
-                        lhsT_scale=x_scales[:, i, h, :],
-                        rhs=words[:, g, :].bitcast(FP8X4),
-                        rhs_scale=planes[4 * (g % PLANES) : P, g // PLANES, :],
-                        start=(h == 0),
-                        stop=(h == X_PASSES - 1),
-                    )
-                banks.append(bank)
-            return banks
+        def project(e, i, words, planes):
+            bank = sums.tile([P, F], F32, tag="sum")
+            for h in range(X_PASSES):
+                g = X_PASSES * e + h
+                nc.tensor.matmul_mx(
+                    out=bank[:],
+                    lhsT=x_codes[:, i, h, :].bitcast(FP8X4),
+                    lhsT_scale=x_scales[:, i, h, :],
+                    rhs=words[:, g, :].bitcast(FP8X4),
+                    rhs_scale=planes[4 * (g % PLANES) : P, g // PLANES, :],
+                    start=(h == 0),
+                    stop=(h == X_PASSES - 1),
+                )
+            return bank
 
-        def mix(e, i, gate, up):
+        def silu_of(gate):
             gate_silu = work.tile([P, 2, P, 2], F32, tag="gate_silu")
             nc.scalar.activation(
                 out=gate_silu[:], in_=gate[:].rearrange("n (p u v) -> n u p v", u=2, v=2), func=SILU
             )
+            return gate_silu
+
+        def mix(e, i, gate_silu, up):
             mixed = mixed_pool.tile([P, 2, P, 2], BF16, tag="mixed")
             for u in range(2):
                 nc.vector.scalar_tensor_tensor(
@@ -231,9 +242,9 @@ def tile_moelayer_pa_e_kernel(
 
         mixed_tiles = {}
         for e in range(E):
+            gate_silus = [silu_of(project(e, i, wg_words, wg_planes)) for i in range(TOKEN_TILES)]
             for i in range(TOKEN_TILES):
-                gate, up = gate_and_up(e, i)
-                mixed_tiles[(e, i)] = mix(e, i, gate, up)
+                mixed_tiles[(e, i)] = mix(e, i, gate_silus[i], project(e, i, wu_words, wu_planes))
             if e >= T_RUN and e % T_RUN == 0:
                 flip_run(list(range(e - T_RUN, e)), ["scalar"] * T_RUN)
 

@@ -37,6 +37,7 @@ def tile_moelayer_pa_e_kernel(
         keep = ctx.enter_context(tc.tile_pool(name="keep", bufs=1))
         work = ctx.enter_context(tc.tile_pool(name="work", bufs=3))
         mixed_pool = ctx.enter_context(tc.tile_pool(name="mixed", bufs=8))
+        rows_pool = ctx.enter_context(tc.tile_pool(name="rows", bufs=6))
         sums = ctx.enter_context(tc.psum_pool(name="sums", bufs=6))
         flips = ctx.enter_context(tc.psum_pool(name="flips", bufs=2))
         ctx.enter_context(tc.manual_schedule())
@@ -68,12 +69,13 @@ def tile_moelayer_pa_e_kernel(
             nc.scalar.dma_start(out=x_rows[:, i, :], in_=x[i])
         nc.scalar.activation(out=table_out[:], in_=table_in[:], func=SILU)
 
-        def load_scale_rows(planes, scales, block, quadrant):
-            nc.sync.dma_start(
-                out=planes[32 * quadrant : 32 * quadrant + PLANES * 4, block, :].bitcast(I32),
+        def load_scale_rows(planes, scales, block, quadrant, on_gpsimd=False):
+            queue, view = (nc.gpsimd, F32) if on_gpsimd else (nc.sync, I32)
+            queue.dma_start(
+                out=planes[32 * quadrant : 32 * quadrant + PLANES * 4, block, :].bitcast(view),
                 in_=scales[
                     PLANES * block : PLANES * (block + 1), 4 * quadrant : 4 * (quadrant + 1), :
-                ].bitcast(I32),
+                ].bitcast(view),
             )
 
         def load_words(words, dram_words, first, count, columns):
@@ -104,7 +106,9 @@ def tile_moelayer_pa_e_kernel(
         for small in small_loads[QUADRANTS : 2 * QUADRANTS]:
             load_scale_rows(*small)
         nc.sync.dma_start(out=r_rows[:], in_=r.rearrange("(i p) e -> p i e", p=P))
-        woven = small_loads[2 * QUADRANTS :]
+        for small in small_loads[4 * QUADRANTS : 8 * QUADRANTS]:
+            load_scale_rows(*small, on_gpsimd=True)
+        woven = small_loads[2 * QUADRANTS : 4 * QUADRANTS] + small_loads[8 * QUADRANTS :]
         for e in range(1, E):
             for words, dram_words, planes, scales in gate_up_weights:
                 load_words(words, dram_words, X_PASSES * e, X_PASSES, slice(0, F))
@@ -219,26 +223,24 @@ def tile_moelayer_pa_e_kernel(
             for e, grouped in zip(experts, grouped_tiles):
                 quantise(e, grouped)
 
-        def down(y, i, half, experts):
-            columns = slice(BANK * half, BANK * (half + 1))
-            for e in experts:
-                nc.tensor.matmul_mx(
-                    out=y[:],
-                    lhsT=w_codes[:, e, i, :].bitcast(FP8X4),
-                    lhsT_scale=w_scales[:, e, i, :],
-                    rhs=wd_words[:, e, columns].bitcast(FP8X4),
-                    rhs_scale=wd_planes[4 * (e % PLANES) : P, e // PLANES, columns],
-                    start=(e == 0),
-                    stop=(e == E - 1),
-                )
+        def down(y, i, columns, e):
+            nc.tensor.matmul_mx(
+                out=y[:],
+                lhsT=w_codes[:, e, i, :].bitcast(FP8X4),
+                lhsT_scale=w_scales[:, e, i, :],
+                rhs=wd_words[:, e, columns].bitcast(FP8X4),
+                rhs_scale=wd_planes[4 * (e % PLANES) : P, e // PLANES, columns],
+                start=(e == 0),
+                stop=(e == E - 1),
+            )
 
-        def store(y, i, half):
-            y_rows = work.tile([P, BANK], F32, tag="y_rows")
-            if i == 0:
+        def store(y, i, columns, engine):
+            y_rows = rows_pool.tile([P, columns.stop - columns.start], F32, tag="y_rows")
+            if engine == "vector":
                 nc.vector.tensor_copy(out=y_rows[:], in_=y[:])
             else:
                 nc.scalar.copy(out=y_rows[:], in_=y[:])
-            nc.sync.dma_start(out=out[i, :, BANK * half : BANK * (half + 1)], in_=y_rows[:])
+            nc.sync.dma_start(out=out[i, :, columns], in_=y_rows[:])
 
         mixed_tiles = {}
         for e in range(E):
@@ -249,15 +251,22 @@ def tile_moelayer_pa_e_kernel(
                 flip_run(list(range(e - T_RUN, e)), ["scalar"] * T_RUN)
 
         flip_before = [4, 5]
+        widths = {0: BANK, 1: BANK // 2}
         for half in range(D_HALVES):
-            y_banks = [
-                sums.tile([P, BANK], F32, tag="sum", name="y%d%d" % (half, i)) for i in range(TOKEN_TILES)
+            pieces = [
+                (i, slice(first, first + widths[half]))
+                for i in range(TOKEN_TILES)
+                for first in range(BANK * half, BANK * (half + 1), widths[half])
+            ]
+            y_tiles = [
+                sums.tile([P, widths[half]], F32, tag="sum", name="y%d_%d" % (half, n))
+                for n in range(len(pieces))
             ]
             for chunk in wd_chunks[half]:
                 if half == 0 and chunk == flip_before:
                     flip_run(list(range(E - T_RUN, E)), ["scalar", "vector"])
                 for e in chunk:
-                    for i in range(TOKEN_TILES):
-                        down(y_banks[i], i, half, [e])
-            for i in range(TOKEN_TILES):
-                store(y_banks[i], i, half)
+                    for y, (i, columns) in zip(y_tiles, pieces):
+                        down(y, i, columns, e)
+            for n, (y, (i, columns)) in enumerate(zip(y_tiles, pieces)):
+                store(y, i, columns, ["vector", "scalar"][n % 2])

@@ -42,18 +42,25 @@ def tile_moelayer_pa_e_kernel(
         flips = ctx.enter_context(tc.psum_pool(name="flips", bufs=2))
         ctx.enter_context(tc.manual_schedule())
 
-        wg_words = keep.tile([P, E * X_PASSES, F], U32, align_bytes=64)
-        wu_words = keep.tile([P, E * X_PASSES, F], U32, align_bytes=64)
-        wd_words = keep.tile([P, E, D], U32, align_bytes=64)
-        wg_planes = keep.tile([P, E * X_PASSES // PLANES, F], U8, align_bytes=64)
-        wu_planes = keep.tile([P, E * X_PASSES // PLANES, F], U8, align_bytes=64)
-        wd_planes = keep.tile([P, E // PLANES, D], U8, align_bytes=64)
+        wg_words = keep.tile([P, E * X_PASSES, F], U32, align_bytes=256)
+        wu_words = keep.tile([P, E * X_PASSES, F], U32, align_bytes=256)
+        wd_words = keep.tile([P, E, D], U32, align_bytes=256)
+        wg_planes_tile = keep.tile([P, 64 + E * X_PASSES // PLANES * F], U8, align_bytes=256)
+        wu_planes_tile = keep.tile([P, 64 + E * X_PASSES // PLANES * F], U8, align_bytes=256)
+        wd_planes_tile = keep.tile([P, 64 + E // PLANES * D], U8, align_bytes=256)
+        wg_planes = wg_planes_tile[:, 64:].rearrange("p (b n) -> p b n", n=F)
+        wu_planes = wu_planes_tile[:, 64:].rearrange("p (b n) -> p b n", n=F)
+        wd_planes = wd_planes_tile[:, 64:].rearrange("p (b n) -> p b n", n=D)
         x_rows = keep.tile([P, TOKEN_TILES, D], BF16)
         x_grouped = keep.tile([P, TOKEN_TILES, X_PASSES, P, PACK], BF16, align_bytes=64)
-        x_codes = keep.tile([P, TOKEN_TILES, X_PASSES, P], U32, align_bytes=64)
-        x_scales = keep.tile([P, TOKEN_TILES, X_PASSES, P], U8, align_bytes=64)
-        w_codes = keep.tile([P, E, TOKEN_TILES, P], U32, align_bytes=64)
-        w_scales = keep.tile([P, E, TOKEN_TILES, P], U8, align_bytes=64)
+        x_codes_tile = keep.tile([P, 32 + TOKEN_TILES * X_PASSES * P], U32, align_bytes=256)
+        x_scales_tile = keep.tile([P, 192 + TOKEN_TILES * X_PASSES * P], U8, align_bytes=256)
+        w_codes_tile = keep.tile([P, 32 + E * TOKEN_TILES * P], U32, align_bytes=256)
+        w_scales_tile = keep.tile([P, 192 + E * TOKEN_TILES * P], U8, align_bytes=256)
+        x_codes = x_codes_tile[:, 32:].rearrange("p (i g n) -> p i g n", i=TOKEN_TILES, g=X_PASSES)
+        x_scales = x_scales_tile[:, 192:].rearrange("p (i g n) -> p i g n", i=TOKEN_TILES, g=X_PASSES)
+        w_codes = w_codes_tile[:, 32:].rearrange("p (e i n) -> p e i n", e=E, i=TOKEN_TILES)
+        w_scales = w_scales_tile[:, 192:].rearrange("p (e i n) -> p e i n", e=E, i=TOKEN_TILES)
         r_rows = keep.tile([P, TOKEN_TILES, E], BF16)
         r_f32 = keep.tile([P, TOKEN_TILES, E], F32)
         ident_f32 = keep.tile([P, P], F32)
@@ -61,8 +68,8 @@ def tile_moelayer_pa_e_kernel(
         table_out = keep.tile([P, 1], F32)
 
         nc.vector.memset(table_in[:], 0.0)
-        for planes in (wg_planes, wu_planes, wd_planes):
-            nc.vector.memset(planes[:].rearrange("p b n -> p (b n)").bitcast(I32), 0)
+        for planes_tile in (wg_planes_tile, wu_planes_tile, wd_planes_tile):
+            nc.vector.memset(planes_tile[:].bitcast(I32), 0)
         make_identity(nc, ident_f32[:])
 
         for i in range(TOKEN_TILES):

@@ -54,9 +54,9 @@ def tile_moelayer_pa_e_kernel(
         x_rows = keep.tile([P, TOKEN_TILES, D], BF16)
         x_grouped = keep.tile([P, TOKEN_TILES, X_PASSES, P, PACK], BF16, align_bytes=64)
         x_codes_tile = keep.tile([P, 32 + TOKEN_TILES * X_PASSES * P], U32, align_bytes=256)
-        x_scales_tile = keep.tile([P, 192 + TOKEN_TILES * X_PASSES * P], U8, align_bytes=256)
+        x_scales_tile = keep.tile([P, 192 + TOKEN_TILES * X_PASSES * 2 * P], U8, align_bytes=256)
         w_codes_tile = keep.tile([P, 32 + E * TOKEN_TILES * P], U32, align_bytes=256)
-        w_scales_tile = keep.tile([P, 192 + E * TOKEN_TILES * P], U8, align_bytes=256)
+        w_scales_tile = keep.tile([P, 192 + E * TOKEN_TILES * 2 * P], U8, align_bytes=256)
         x_codes = x_codes_tile[:, 32:].rearrange("p (i g n) -> p i g n", i=TOKEN_TILES, g=X_PASSES)
         x_scales = x_scales_tile[:, 192:].rearrange("p (i g n) -> p i g n", i=TOKEN_TILES, g=X_PASSES)
         w_codes = w_codes_tile[:, 32:].rearrange("p (e i n) -> p e i n", e=E, i=TOKEN_TILES)
@@ -155,11 +155,12 @@ def tile_moelayer_pa_e_kernel(
             else:
                 nc.scalar.copy(out=grouped_pairs, in_=x_flipped[:].rearrange("p g u n -> p g n u"))
         for i in range(TOKEN_TILES):
-            nc.vector.quantize_mx(
-                out=x_codes[:, i].rearrange("p g n -> p (g n)").bitcast(FP8X4),
-                scales=x_scales[:, i].rearrange("p g n -> p (g n)"),
-                in_=x_grouped[:, i].rearrange("p g n t -> p (g n t)"),
-            )
+            for g in range(X_PASSES):
+                nc.vector.quantize_mx(
+                    out=x_codes[:, i, g, :].bitcast(FP8X4),
+                    scales=x_scales[:, i, g, 0:P],
+                    in_=x_grouped[:, i, g].rearrange("p n t -> p (n t)"),
+                )
         nc.vector.tensor_copy(out=r_f32[:], in_=r_rows[:])
 
         def project(e, i, words, planes):
@@ -169,7 +170,7 @@ def tile_moelayer_pa_e_kernel(
                 nc.tensor.matmul_mx(
                     out=bank[:],
                     lhsT=x_codes[:, i, h, :].bitcast(FP8X4),
-                    lhsT_scale=x_scales[:, i, h, :],
+                    lhsT_scale=x_scales[:, i, h, 0:P],
                     rhs=words[:, g, :].bitcast(FP8X4),
                     rhs_scale=planes[4 * (g % PLANES) : P, g // PLANES, :],
                     start=(h == 0),
@@ -219,11 +220,12 @@ def tile_moelayer_pa_e_kernel(
             return grouped
 
         def quantise(e, grouped):
-            nc.vector.quantize_mx(
-                out=w_codes[:, e].rearrange("p i n -> p (i n)").bitcast(FP8X4),
-                scales=w_scales[:, e].rearrange("p i n -> p (i n)"),
-                in_=grouped[:].rearrange("p i n t -> p (i n t)"),
-            )
+            for i in range(TOKEN_TILES):
+                nc.vector.quantize_mx(
+                    out=w_codes[:, e, i, :].bitcast(FP8X4),
+                    scales=w_scales[:, e, i, 0:P],
+                    in_=grouped[:, i].rearrange("p n t -> p (n t)"),
+                )
 
         def flip_run(experts, copy_engines):
             grouped_tiles = [flip_and_quantise(e, engine) for e, engine in zip(experts, copy_engines)]
@@ -234,7 +236,7 @@ def tile_moelayer_pa_e_kernel(
             nc.tensor.matmul_mx(
                 out=y[:],
                 lhsT=w_codes[:, e, i, :].bitcast(FP8X4),
-                lhsT_scale=w_scales[:, e, i, :],
+                lhsT_scale=w_scales[:, e, i, 0:P],
                 rhs=wd_words[:, e, columns].bitcast(FP8X4),
                 rhs_scale=wd_planes[4 * (e % PLANES) : P, e // PLANES, columns],
                 start=(e == 0),

from contextlib import ExitStack

import concourse.mybir as mybir
from concourse.masks import make_identity

F32 = mybir.dt.float32
BF16 = mybir.dt.bfloat16
I32 = mybir.dt.int32
U32 = mybir.dt.uint32
U8 = mybir.dt.uint8
FP8X4 = mybir.dt.float8_e4m3fn_x4
SILU = mybir.ActivationFunctionType.Silu
MULT = mybir.AluOpType.mult

P = 128
PACK = 4
K_PASS = P * PACK
TOKEN_TILES = 2
D = 1024
E = 8
F = 512
X_PASSES = D // K_PASS
BANK = 512
D_HALVES = D // BANK
QUADRANTS = 4
T_RUN = 2
PLANES = 4

FLOPS = 2 * TOKEN_TILES * P * E * (2 * D * F + F * D)


def tile_moelayer_pa_e_kernel(
    tc, x, r, Wg_words, Wg_scales, Wu_words, Wu_scales, Wd_words, Wd_scales, out
):
    nc = tc.nc
    with ExitStack() as ctx:
        keep = ctx.enter_context(tc.tile_pool(name="keep", bufs=1))
        work = ctx.enter_context(tc.tile_pool(name="work", bufs=3))
        mixed_pool = ctx.enter_context(tc.tile_pool(name="mixed", bufs=8))
        rows_pool = ctx.enter_context(tc.tile_pool(name="rows", bufs=6))
        sums = ctx.enter_context(tc.psum_pool(name="sums", bufs=6))
        flips = ctx.enter_context(tc.psum_pool(name="flips", bufs=2))
        ctx.enter_context(tc.manual_schedule())

        wg_words = keep.tile([P, E * X_PASSES, F], U32, align_bytes=256)
        wu_words = keep.tile([P, E * X_PASSES, F], U32, align_bytes=256)
        wd_words = keep.tile([P, E, D], U32, align_bytes=256)
        wg_planes_tile = keep.tile([P, 64 + E * X_PASSES // PLANES * F], U8, align_bytes=256)
        wu_planes_tile = keep.tile([P, 64 + E * X_PASSES // PLANES * F], U8, align_bytes=256)
        wd_planes_tile = keep.tile([P, 64 + E // PLANES * D], U8, align_bytes=256)
        wg_planes = wg_planes_tile[:, 64:].rearrange("p (b n) -> p b n", n=F)
        wu_planes = wu_planes_tile[:, 64:].rearrange("p (b n) -> p b n", n=F)
        wd_planes = wd_planes_tile[:, 64:].rearrange("p (b n) -> p b n", n=D)
        x_rows = keep.tile([P, TOKEN_TILES, D], BF16)
        x_grouped = keep.tile([P, TOKEN_TILES, X_PASSES, P, PACK], BF16, align_bytes=64)
        x_codes_tile = keep.tile([P, 32 + TOKEN_TILES * X_PASSES * P], U32, align_bytes=256)
        x_scales_tile = keep.tile([P, 192 + TOKEN_TILES * X_PASSES * 2 * P], U8, align_bytes=256)
        w_codes_tile = keep.tile([P, 32 + E * TOKEN_TILES * P], U32, align_bytes=256)
        w_scales_tile = keep.tile([P, 192 + E * TOKEN_TILES * 2 * P], U8, align_bytes=256)
        x_codes = x_codes_tile[:, 32:].rearrange("p (i g n) -> p i g n", i=TOKEN_TILES, g=X_PASSES)
        x_scales = x_scales_tile[:, 192:].rearrange("p (i g n) -> p i g n", i=TOKEN_TILES, g=X_PASSES)
        w_codes = w_codes_tile[:, 32:].rearrange("p (e i n) -> p e i n", e=E, i=TOKEN_TILES)
        w_scales = w_scales_tile[:, 192:].rearrange("p (e i n) -> p e i n", e=E, i=TOKEN_TILES)
        r_rows = keep.tile([P, TOKEN_TILES, E], BF16)
        r_f32 = keep.tile([P, TOKEN_TILES, E], F32)
        ident_f32 = keep.tile([P, P], F32)
        table_in = keep.tile([P, 1], F32)
        table_out = keep.tile([P, 1], F32)

        nc.vector.memset(table_in[:], 0.0)
        for planes_tile in (wg_planes_tile, wu_planes_tile, wd_planes_tile):
            nc.vector.memset(planes_tile[:].bitcast(I32), 0)
        make_identity(nc, ident_f32[:])

        for i in range(TOKEN_TILES):
            nc.scalar.dma_start(out=x_rows[:, i, :], in_=x[i])
        nc.scalar.activation(out=table_out[:], in_=table_in[:], func=SILU)

        def load_scale_rows(planes, scales, block, quadrant, on_gpsimd=False):
            queue, view = (nc.gpsimd, F32) if on_gpsimd else (nc.sync, I32)
            queue.dma_start(
                out=planes[32 * quadrant : 32 * quadrant + PLANES * 4, block, :].bitcast(view),
                in_=scales[
                    PLANES * block : PLANES * (block + 1), 4 * quadrant : 4 * (quadrant + 1), :
                ].bitcast(view),
            )

        def load_words(words, dram_words, first, count, columns):
            nc.sync.dma_start(
                out=words[:, first : first + count, columns].bitcast(I32),
                in_=dram_words[first : first + count, :, columns, :]
                .rearrange("g p n t -> p g (n t)")
                .bitcast(I32),
            )

        gate_up_weights = (
            (wg_words, Wg_words, wg_planes, Wg_scales),
            (wu_words, Wu_words, wu_planes, Wu_scales),
        )
        experts_per_block = PLANES // X_PASSES
        small_loads = []
        for block in range(E // experts_per_block):
            for words, dram_words, planes, scales in gate_up_weights:
                for quadrant in range(QUADRANTS):
                    small_loads.append((planes, scales, block, quadrant))
        for block in range(E // PLANES):
            for quadrant in range(QUADRANTS):
                small_loads.append((wd_planes, Wd_scales, block, quadrant))
        for small in small_loads[:QUADRANTS]:
            load_scale_rows(*small)
        for words, dram_words, planes, scales in gate_up_weights:
            load_words(words, dram_words, 0, X_PASSES, slice(0, F))
        for small in small_loads[QUADRANTS : 2 * QUADRANTS]:
            load_scale_rows(*small)
        nc.sync.dma_start(out=r_rows[:], in_=r.rearrange("(i p) e -> p i e", p=P))
        for small in small_loads[4 * QUADRANTS : 8 * QUADRANTS]:
            load_scale_rows(*small, on_gpsimd=True)
        woven = small_loads[2 * QUADRANTS : 4 * QUADRANTS] + small_loads[8 * QUADRANTS :]
        for e in range(1, E):
            for words, dram_words, planes, scales in gate_up_weights:
                load_words(words, dram_words, X_PASSES * e, X_PASSES, slice(0, F))
                for small in woven[:2]:
                    load_scale_rows(*small)
                woven = woven[2:]
        for small in woven:
            load_scale_rows(*small)
        wd_chunks = {
            0: [[0, 1], [2, 3], [4, 5], [6, 7]],
            1: [[0, 1], [2, 3], [4, 5], [6], [7]],
        }
        for half in range(D_HALVES):
            for chunk in wd_chunks[half]:
                load_words(wd_words, Wd_words, chunk[0], len(chunk), slice(BANK * half, BANK * (half + 1)))

        for i in range(TOKEN_TILES):
            x_pairs = x_rows[:, i, :].bitcast(F32)
            x_flipped = flips.tile([P, X_PASSES, 2, P], F32, tag="flip")
            for g in range(X_PASSES):
                for u in range(2):
                    nc.tensor.transpose(
                        x_flipped[:, g, u, :],
                        x_pairs[:, 256 * g + u : 256 * (g + 1) : 2],
                        ident_f32[:],
                    )
            grouped_pairs = (
                x_grouped[:, i]
                .rearrange("p g n t -> p (g n t)")
                .bitcast(F32)
                .rearrange("p (g n u) -> p g n u", g=X_PASSES, u=2)
            )
            if i == 0:
                nc.vector.tensor_copy(
                    out=grouped_pairs, in_=x_flipped[:].rearrange("p g u n -> p g n u")
                )
            else:
                nc.scalar.copy(out=grouped_pairs, in_=x_flipped[:].rearrange("p g u n -> p g n u"))
        for i in range(TOKEN_TILES):
            for g in range(X_PASSES):
                nc.vector.quantize_mx(
                    out=x_codes[:, i, g, :].bitcast(FP8X4),
                    scales=x_scales[:, i, g, 0:P],
                    in_=x_grouped[:, i, g].rearrange("p n t -> p (n t)"),
                )
        nc.vector.tensor_copy(out=r_f32[:], in_=r_rows[:])

        def project(e, i, words, planes):
            bank = sums.tile([P, F], F32, tag="sum")
            for h in range(X_PASSES):
                g = X_PASSES * e + h
                nc.tensor.matmul_mx(
                    out=bank[:],
                    lhsT=x_codes[:, i, h, :].bitcast(FP8X4),
                    lhsT_scale=x_scales[:, i, h, 0:P],
                    rhs=words[:, g, :].bitcast(FP8X4),
                    rhs_scale=planes[4 * (g % PLANES) : P, g // PLANES, :],
                    start=(h == 0),
                    stop=(h == X_PASSES - 1),
                )
            return bank

        def silu_of(gate):
            gate_silu = work.tile([P, 2, P, 2], F32, tag="gate_silu")
            nc.scalar.activation(
                out=gate_silu[:], in_=gate[:].rearrange("n (p u v) -> n u p v", u=2, v=2), func=SILU
            )
            return gate_silu

        def mix(e, i, gate_silu, up):
            mixed = mixed_pool.tile([P, 2, P, 2], BF16, tag="mixed")
            for u in range(2):
                nc.vector.scalar_tensor_tensor(
                    out=mixed[:, u],
                    in0=up[:].rearrange("n (p u v) -> n u p v", u=2, v=2)[:, u],
                    scalar=r_f32[:, i, e : e + 1],
                    in1=gate_silu[:, u],
                    op0=MULT,
                    op1=MULT,
                )
            return mixed

        def flip_and_quantise(e, copy_engine):
            flipped = flips.tile([P, TOKEN_TILES, 2, P], F32, tag="flip")
            for i in range(TOKEN_TILES):
                mixed_pairs = mixed_tiles[(e, i)][:].rearrange("n u p v -> n (u p v)").bitcast(F32)
                for u in range(2):
                    nc.tensor.transpose(
                        flipped[:, i, u, :], mixed_pairs[:, P * u : P * (u + 1)], ident_f32[:]
                    )
            grouped = work.tile([P, TOKEN_TILES, P, PACK], BF16, tag="grouped", align_bytes=64)
            grouped_pairs = (
                grouped[:]
                .rearrange("p i n t -> p (i n t)")
                .bitcast(F32)
                .rearrange("p (i n u) -> p i n u", i=TOKEN_TILES, u=2)
            )
            if copy_engine == "scalar":
                nc.scalar.copy(out=grouped_pairs, in_=flipped[:].rearrange("p i u n -> p i n u"))
            else:
                nc.vector.tensor_copy(out=grouped_pairs, in_=flipped[:].rearrange("p i u n -> p i n u"))
            return grouped

        def quantise(e, grouped):
            for i in range(TOKEN_TILES):
                nc.vector.quantize_mx(
                    out=w_codes[:, e, i, :].bitcast(FP8X4),
                    scales=w_scales[:, e, i, 0:P],
                    in_=grouped[:, i].rearrange("p n t -> p (n t)"),
                )

        def flip_run(experts, copy_engines):
            grouped_tiles = [flip_and_quantise(e, engine) for e, engine in zip(experts, copy_engines)]
            for e, grouped in zip(experts, grouped_tiles):
                quantise(e, grouped)

        def down(y, i, columns, e):
            nc.tensor.matmul_mx(
                out=y[:],
                lhsT=w_codes[:, e, i, :].bitcast(FP8X4),
                lhsT_scale=w_scales[:, e, i, 0:P],
                rhs=wd_words[:, e, columns].bitcast(FP8X4),
                rhs_scale=wd_planes[4 * (e % PLANES) : P, e // PLANES, columns],
                start=(e == 0),
                stop=(e == E - 1),
            )

        def store(y, i, columns, engine):
            y_rows = rows_pool.tile([P, columns.stop - columns.start], F32, tag="y_rows")
            if engine == "vector":
                nc.vector.tensor_copy(out=y_rows[:], in_=y[:])
            else:
                nc.scalar.copy(out=y_rows[:], in_=y[:])
            nc.sync.dma_start(out=out[i, :, columns], in_=y_rows[:])

        mixed_tiles = {}
        for e in range(E):
            gate_silus = [silu_of(project(e, i, wg_words, wg_planes)) for i in range(TOKEN_TILES)]
            for i in range(TOKEN_TILES):
                mixed_tiles[(e, i)] = mix(e, i, gate_silus[i], project(e, i, wu_words, wu_planes))
            if e >= T_RUN and e % T_RUN == 0:
                flip_run(list(range(e - T_RUN, e)), ["scalar"] * T_RUN)

        flip_before = [4, 5]
        widths = {0: BANK, 1: BANK // 2}
        for half in range(D_HALVES):
            pieces = [
                (i, slice(first, first + widths[half]))
                for i in range(TOKEN_TILES)
                for first in range(BANK * half, BANK * (half + 1), widths[half])
            ]
            y_tiles = [
                sums.tile([P, widths[half]], F32, tag="sum", name="y%d_%d" % (half, n))
                for n in range(len(pieces))
            ]
            for chunk in wd_chunks[half]:
                if half == 0 and chunk == flip_before:
                    flip_run(list(range(E - T_RUN, E)), ["scalar", "vector"])
                for e in chunk:
                    for y, (i, columns) in zip(y_tiles, pieces):
                        down(y, i, columns, e)
            for n, (y, (i, columns)) in enumerate(zip(y_tiles, pieces)):
                store(y, i, columns, ["vector", "scalar"][n % 2])
